import numpy as np
import ml_dtypes


def mxq(x, axis, fmt="e4m3"):
    dtype, down = {"e4m3": (ml_dtypes.float8_e4m3fn, 7), "e5m2": (ml_dtypes.float8_e5m2, 14)}[fmt]
    v = np.moveaxis(np.asarray(x, np.float32).astype(ml_dtypes.bfloat16).astype(np.float64), axis, -1)
    blocks = v.reshape(v.shape[:-1] + (-1, 32))
    amax = np.abs(blocks).max(-1, keepdims=True)
    byte = np.maximum(np.where(amax > 0, np.frexp(amax)[1] - 1 + 127, 0) - down, 1)
    scale = np.exp2(byte - 127.0)
    codes = (blocks / scale).astype(np.float32).astype(dtype).astype(np.float64)
    return np.moveaxis((codes * scale).reshape(v.shape), -1, axis)


WIDE = False


def mx_kscale(k):
    if not WIDE:
        return np.ones(k)
    levels = np.array([10, -10, 5, -5, 0])
    if k % 512:
        return np.exp2(np.random.permutation(np.resize(levels, k // 32))).repeat(32)
    a = np.empty((k // 512, 16))
    for p in range(k // 512):
        a[p, :8] = np.random.permutation(np.resize(levels, 8))
        for g in range(8):
            far = levels[np.abs(levels - a[p, g]) >= 10]
            a[p, g + 8] = far[np.random.randint(len(far))]
    return np.exp2(a.ravel()).repeat(32)


BF16 = ml_dtypes.bfloat16


def bf(x):
    return np.asarray(x, np.float32).astype(BF16)


def f64(x):
    return np.asarray(x).astype(np.float64)


N, E, C, D1, D2 = 1024, 2048, 512, 2, 2
T2 = D2 + 1


def shift_down(y, k):
    return np.pad(y, ((k, 0), (0, 0)))[:y.shape[0]] if k > 0 else y


def log_softmax(z):
    d = z - z.max(-1, keepdims=True)
    return d - np.log(np.exp(d).sum(-1, keepdims=True))


def draw0():
    s = mx_kscale(C)
    return {"H": bf(np.tanh(np.random.standard_normal((N, C))) * s),
            "W2": bf(np.random.standard_normal((T2, C, C)) * 2.0 / np.sqrt(C) / s[None, :, None]),
            "b2": bf(np.random.standard_normal((1, C)) * 0.2)}


def core(H, W2, b2):
    G = mxq(f64(H), 1, "e4m3") @ mxq(f64(W2), 1, "e4m3")
    Z = sum(shift_down(G[j], D2 - j) for j in range(T2)) + T2 * f64(b2)[0]
    return log_softmax(Z)


def e4m3fn_bytes(y):
    return np.clip(np.asarray(y, np.float64), -448.0, 448.0).astype(np.float32).astype(ml_dtypes.float8_e4m3fn).view(np.uint8)


def e4m3fn_values(b):
    return np.asarray(b, np.uint8).view(ml_dtypes.float8_e4m3fn).astype(np.float64)


def setup_inputs():
    d = draw0()
    x0 = np.asarray(d['W2']).astype(np.float64)
    s = (np.max(np.abs(x0), axis=(0, 2), keepdims=True) / 448.0).astype(np.float32)
    out = {}
    for k, v in d.items():
        if k == 'W2':
            out['W2_bytes'] = e4m3fn_bytes(x0 / s.astype(np.float64))
            out['W2_scale'] = s
        else:
            out[k] = v
    return out


def reference(H, W2_bytes, W2_scale, b2):
    return core(H, e4m3fn_values(W2_bytes) * W2_scale.astype(np.float64), b2)

@@ -1,0 +1,269 @@
+from contextlib import ExitStack
+import math
+
+import concourse.mybir as mybir
+from concourse.masks import make_identity
+
+N_TOK, K_DIM, N_CLS, TAPS = 1024, 512, 512, 3
+FLOPS = 2 * N_TOK * K_DIM * N_CLS * TAPS
+
+F32 = mybir.dt.float32
+BF16 = mybir.dt.bfloat16
+U32 = mybir.dt.uint32
+U8 = mybir.dt.uint8
+FP8 = mybir.dt.float8_e4m3fn
+FP8X4 = mybir.dt.float8_e4m3fn_x4
+ACT = mybir.ActivationFunctionType
+ALU = mybir.AluOpType
+AX = mybir.AxisListType
+
+P = 128
+SLOTS = 8
+
+LN_A = math.log(2.0) / 8388608.0
+LN_B = (0.043036986972427194 - 127.0) * math.log(2.0)
+LN_C = (
+    -1.0, 0.5, -0.3333333432674408, 0.2500000596046448, -0.19999957084655762, 0.16666363179683685,
+    -0.14286194741725922, 0.12505744397640228, -0.11113137751817703, 0.09948977828025818, -0.0901292935013771,
+    0.08533929288387299, -0.08288848400115967, 0.07088949531316757, -0.04805668443441391, 0.04240668565034866,
+    -0.07241664826869965, 0.10330895334482193, -0.0916367769241333, 0.04873454570770264, -0.014420325867831707,
+    0.0018373848870396614,
+)
+DEG = len(LN_C)
+S_FINALS = 4
+
+
+def tile_predictor_pb_kernel(tc, H, W2_bytes, W2_scale, b2, out):
+    nc = tc.nc
+    h_view = H.rearrange("(q r) k -> q r k", r=SLOTS)
+    out_view = out.rearrange("(q r) c -> q r c", r=SLOTS)
+
+    with ExitStack() as ctx:
+        keep = ctx.enter_context(tc.tile_pool(name="keep", bufs=1))
+        scrap = ctx.enter_context(tc.tile_pool(name="scrap", bufs=2))
+        ps_t = ctx.enter_context(tc.psum_pool(name="ps_t", bufs=4))
+        ps_a = ctx.enter_context(tc.psum_pool(name="ps_a", bufs=4))
+        ctx.enter_context(tc.manual_schedule())
+
+        ident = keep.tile([P, P], F32, name="ident")
+        b2b = keep.tile([P, N_CLS], BF16, name="b2b")
+        wsc = keep.tile([P, 4], F32, name="wsc")
+        warm = keep.tile([P, 1], F32, name="warm")
+        warm2 = keep.tile([P, 1], F32, name="warm2")
+        w_bytes = [keep.tile([P, 4 * N_CLS], U8, name="w_bytes%d" % j) for j in range(TAPS)]
+        w_wide = [keep.tile([P, 4 * N_CLS], BF16, name="w_wide%d" % j) for j in range(TAPS)]
+        w_grp = [keep.tile([P, 4 * N_CLS], BF16, name="w_grp%d" % j, align_bytes=64) for j in range(TAPS)]
+        w_codes = [keep.tile([P, N_CLS], U32, name="w_codes%d" % j, align_bytes=64) for j in range(TAPS)]
+        w_scl = [keep.tile([P, N_CLS], U8, name="w_scl%d" % j, align_bytes=64) for j in range(TAPS)]
+        hs = keep.tile([P, SLOTS, K_DIM], BF16, name="hs")
+        hg = keep.tile([P, (SLOTS + 2) * K_DIM], BF16, name="hg", align_bytes=64)
+        h_codes = keep.tile([P, (SLOTS + 2) * P], U32, name="h_codes", align_bytes=64)
+        h_scl = keep.tile([P, (SLOTS + 2) * P], U8, name="h_scl", align_bytes=64)
+        zt = keep.tile([P, SLOTS, N_CLS], F32, name="zt")
+        nmax = keep.tile([P, SLOTS], F32, name="nmax")
+        ssum = keep.tile([P, SLOTS], F32, name="ssum")
+        e_inv = keep.tile([P, SLOTS], F32, name="e_inv")
+        ny0 = keep.tile([P, SLOTS], F32, name="ny0")
+        u_t = keep.tile([P, SLOTS], F32, name="u_t")
+        coef = keep.tile([P, SLOTS, DEG], F32, name="coef")
+        horn = keep.tile([P, SLOTS, DEG], F32, name="horn")
+
+        def load_w(j, t0, t1):
+            nc.sync.dma_start(
+                out=w_bytes[j][:, t0 * N_CLS : t1 * N_CLS],
+                in_=W2_bytes[j, :, :].rearrange("(p t) n -> p (t n)", t=4)[:, t0 * N_CLS : t1 * N_CLS],
+            )
+
+        def load_h(b):
+            nc.sync.dma_start(out=hs[:, 2 * b : 2 * b + 2, :], in_=h_view[:, 2 * b : 2 * b + 2, :])
+
+        def widen(eng, j, t):
+            cols = slice(t * N_CLS, (t + 1) * N_CLS)
+            src = w_bytes[j][:, cols].bitcast(FP8)
+            if eng == "s":
+                nc.scalar.activation(out=w_wide[j][:, cols], in_=src, func=ACT.Copy, scale=wsc[:, t : t + 1])
+            else:
+                nc.vector.tensor_scalar(
+                    out=w_wide[j][:, cols], in0=src, scalar1=wsc[:, t : t + 1], scalar2=None, op0=ALU.mult
+                )
+
+        def interleave(j):
+            nc.vector.tensor_copy(
+                out=w_grp[j][:].rearrange("p (n t) -> p n t", t=4),
+                in_=w_wide[j][:].rearrange("p (t n) -> p n t", t=4),
+            )
+
+        def quant_w(j):
+            nc.vector.quantize_mx(out=w_codes[j][:].bitcast(FP8X4), scales=w_scl[j][:], in_=w_grp[j][:])
+
+        tps = {}
+
+        def transposes(b):
+            tp = ps_t.tile([P, 2, 2, P], F32, tag="tp", name="tp%d" % b)
+            tps[b] = tp
+            for s in range(2):
+                words = hs[:, 2 * b + s, :].bitcast(F32)
+                for u in range(2):
+                    nc.tensor.transpose(out=tp[:, s, u, :], in_=words[:, u : K_DIM // 2 : 2], identity=ident[:])
+
+        def evac_h(b):
+            e0 = 2 + 2 * b
+            dst = hg[:, e0 * K_DIM : (e0 + 2) * K_DIM].bitcast(F32).rearrange("p (s q u) -> p s q u", s=2, u=2)
+            nc.scalar.copy(out=dst, in_=tps[b][:].rearrange("p s u q -> p s q u"))
+
+        def evac_shift():
+            dst = hg[:, 0 : 2 * K_DIM].bitcast(F32).rearrange("p (s q u) -> p s q u", s=2, u=2)
+            src = tps[3][:].rearrange("p s u q -> p s q u")
+            nc.scalar.copy(out=dst[:, :, 1:P, :], in_=src[:, :, 0 : P - 1, :])
+
+        def quant_h(e0, n):
+            nc.vector.quantize_mx(
+                out=h_codes[:, e0 * P : (e0 + n) * P].bitcast(FP8X4),
+                scales=h_scl[:, e0 * P : (e0 + n) * P],
+                in_=hg[:, e0 * K_DIM : (e0 + n) * K_DIM],
+            )
+
+        accs = {}
+
+        def mm(i, j, first, last):
+            if first:
+                accs[i] = ps_a.tile([P, N_CLS], F32, tag="acc", name="acc%d" % i)
+            e = (i + 2) % SLOTS + j
+            nc.tensor.matmul_mx(
+                out=accs[i][:],
+                lhsT=h_codes[:, e * P : (e + 1) * P].bitcast(FP8X4),
+                lhsT_scale=h_scl[:, e * P : (e + 1) * P],
+                rhs=w_codes[j][:].bitcast(FP8X4),
+                rhs_scale=w_scl[j][:],
+                start=first,
+                stop=last,
+            )
+
+        def tile_mms(i):
+            for j in range(TAPS):
+                mm(i, j, j == 0, j == TAPS - 1)
+
+        def add_bias(i):
+            r = (i + 2) % SLOTS
+            nc.vector.scalar_tensor_tensor(
+                out=zt[:, r, :], in0=b2b[:], scalar=3.0, in1=accs[i][:], op0=ALU.mult, op1=ALU.add
+            )
+
+        def row_max(i):
+            r = (i + 2) % SLOTS
+            nc.vector.tensor_reduce(out=nmax[:, i : i + 1], in_=zt[:, r, :], axis=AX.X, op=ALU.max, negate=True)
+
+        def exp_sum(i):
+            r = (i + 2) % SLOTS
+            ex = scrap.tile([P, N_CLS], BF16, tag="ex", name="ex%d" % i)
+            nc.scalar.activation(
+                out=ex[:], in_=zt[:, r, :], func=ACT.Exp, bias=nmax[:, i : i + 1], scale=1.0,
+                accum_out=ssum[:, i : i + 1],
+            )
+
+        def ln_guess(i):
+            c = slice(i, i + 1)
+            bits = ssum[:, c].bitcast(U32)
+            nc.scalar.activation(out=e_inv[:, c], in_=bits, func=ACT.Exp, bias=-LN_B, scale=-LN_A)
+            nc.scalar.activation(out=ny0[:, c], in_=bits, func=ACT.Identity, bias=-LN_B, scale=-LN_A)
+            nc.gpsimd.tensor_tensor(out=coef[:, i, DEG - 1 : DEG], in0=nmax[:, c], in1=ny0[:, c], op=ALU.add)
+
+        def ln_rest(i):
+            c = slice(i, i + 1)
+            nc.scalar.activation(out=u_t[:, c], in_=e_inv[:, c], func=ACT.Copy, bias=-1.0, scale=ssum[:, c])
+
+        def ln_horner(i):
+            nc.vector.tensor_tensor_scan(
+                out=horn[:, i, :], data0=u_t[:, i : i + 1].to_broadcast([P, DEG]), data1=coef[:, i, :],
+                initial=LN_C[DEG - 1], op0=ALU.mult, op1=ALU.add,
+            )
+
+        def final(eng, i):
+            r = (i + 2) % SLOTS
+            negc = horn[:, i, DEG - 1 : DEG]
+            if eng == "s":
+                nc.scalar.activation(out=zt[:, r, :], in_=zt[:, r, :], func=ACT.Identity, bias=negc, scale=1.0)
+            elif eng == "g":
+                nc.gpsimd.tensor_scalar(
+                    out=zt[:, r, :], in0=zt[:, r, :], scalar1=1.0, scalar2=negc, op0=ALU.mult, op1=ALU.add
+                )
+            else:
+                nc.vector.tensor_scalar(out=zt[:, r, :], in0=zt[:, r, :], scalar1=negc, scalar2=None, op0=ALU.add)
+            nc.sync.dma_start(out=out_view[:, r, :], in_=zt[:, r, :])
+
+        nc.scalar.dma_start(out=wsc[:], in_=W2_scale[0, :, :].rearrange("(p t) u -> p (t u)", t=4))
+        load_w(0, 0, 2)
+        load_w(0, 2, 4)
+        load_w(1, 0, 4)
+        load_h(0)
+        load_h(1)
+        load_w(2, 0, 4)
+        load_h(2)
+        load_h(3)
+        nc.sync.dma_start(out=b2b[:], in_=b2.rearrange("o c -> (o c)").partition_broadcast(P))
+        nc.gpsimd.memset(warm[:], 0.0)
+        make_identity(nc, ident[:])
+        nc.vector.memset(hg[:, 0 : 2 * K_DIM], 0.0)
+        nc.scalar.activation(out=warm2[:], in_=warm[:], func=ACT.Exp)
+        for t in range(DEG - 1):
+            nc.gpsimd.memset(coef[:, :, t], LN_C[DEG - 2 - t])
+
+        widen("s", 0, 0)
+        widen("v", 0, 1)
+        widen("v", 0, 2)
+        widen("v", 0, 3)
+        widen("v", 1, 3)
+        transposes(0)
+        transposes(1)
+        for t in range(3):
+            widen("s", 1, t)
+        interleave(0)
+        widen("v", 2, 3)
+        transposes(2)
+        transposes(3)
+        evac_h(0)
+        evac_h(1)
+        interleave(1)
+        quant_w(0)
+        for t in range(3):
+            widen("s", 2, t)
+        quant_h(2, 4)
+        quant_w(1)
+        for i in range(3):
+            mm(i, 0, True, False)
+        for i in range(3):
+            mm(i, 1, False, False)
+        evac_h(2)
+        evac_h(3)
+        evac_shift()
+        interleave(2)
+        quant_h(6, 2)
+        quant_w(2)
+        for i in range(3):
+            mm(i, 2, False, True)
+        quant_h(8, 2)
+        quant_h(0, 2)
+        tile_mms(3)
+
+        add_bias(0)
+        for i in range(SLOTS):
+            if i + 1 < SLOTS:
+                add_bias(i + 1)
+            row_max(i)
+            if i + 4 < SLOTS:
+                tile_mms(i + 4)
+            if i >= 2:
+                ln_horner(i - 2)
+            exp_sum(i)
+            if i >= 1:
+                ln_rest(i - 1)
+            if 0 <= i - 2 < S_FINALS:
+                final("s", i - 2)
+            ln_guess(i)
+        ln_rest(SLOTS - 1)
+        for k in range(S_FINALS, SLOTS - 2):
+            final("v", k)
+        ln_horner(SLOTS - 2)
+        final("v", SLOTS - 2)
+        ln_horner(SLOTS - 1)
+        final("v", SLOTS - 1)

@@ -30,7 +30,8 @@ LN_C = (
     0.0018373848870396614,
 )
 DEG = len(LN_C)
-S_FINALS = 4
+S_FINALS = 3
+SPLIT = 192
 
 
 def tile_predictor_pb_kernel(tc, H, W2_bytes, W2_scale, b2, out):
@@ -89,8 +90,8 @@ def tile_predictor_pb_kernel(tc, H, W2_bytes, W2_scale, b2, out):
 
         def interleave(j):
             nc.vector.tensor_copy(
-                out=w_grp[j][:].rearrange("p (n t) -> p n t", t=4),
-                in_=w_wide[j][:].rearrange("p (t n) -> p n t", t=4),
+                out=w_grp[j][:].rearrange("p (c i t) -> p c t i", i=4, t=4),
+                in_=w_wide[j][:].rearrange("p (t c i) -> p c t i", t=4, i=4),
             )
 
         def quant_w(j):
@@ -161,16 +162,18 @@ def tile_predictor_pb_kernel(tc, H, W2_bytes, W2_scale, b2, out):
                 accum_out=ssum[:, i : i + 1],
             )
 
-        def ln_guess(i):
-            c = slice(i, i + 1)
+        def ln_guess(i0, i1):
+            c = slice(i0, i1)
             bits = ssum[:, c].bitcast(U32)
             nc.scalar.activation(out=e_inv[:, c], in_=bits, func=ACT.Exp, bias=-LN_B, scale=-LN_A)
             nc.scalar.activation(out=ny0[:, c], in_=bits, func=ACT.Identity, bias=-LN_B, scale=-LN_A)
-            nc.gpsimd.tensor_tensor(out=coef[:, i, DEG - 1 : DEG], in0=nmax[:, c], in1=ny0[:, c], op=ALU.add)
 
         def ln_rest(i):
             c = slice(i, i + 1)
             nc.scalar.activation(out=u_t[:, c], in_=e_inv[:, c], func=ACT.Copy, bias=-1.0, scale=ssum[:, c])
+            nc.scalar.activation(
+                out=coef[:, i, DEG - 1 : DEG], in_=nmax[:, c], func=ACT.Identity, bias=ny0[:, c], scale=1.0
+            )
 
         def ln_horner(i):
             nc.vector.tensor_tensor_scan(
@@ -178,18 +181,21 @@ def tile_predictor_pb_kernel(tc, H, W2_bytes, W2_scale, b2, out):
                 initial=LN_C[DEG - 1], op0=ALU.mult, op1=ALU.add,
             )
 
-        def final(eng, i):
+        def final(eng, i, c0=0, c1=N_CLS):
             r = (i + 2) % SLOTS
             negc = horn[:, i, DEG - 1 : DEG]
             if eng == "s":
-                nc.scalar.activation(out=zt[:, r, :], in_=zt[:, r, :], func=ACT.Identity, bias=negc, scale=1.0)
-            elif eng == "g":
-                nc.gpsimd.tensor_scalar(
-                    out=zt[:, r, :], in0=zt[:, r, :], scalar1=1.0, scalar2=negc, op0=ALU.mult, op1=ALU.add
+                nc.scalar.activation(
+                    out=zt[:, r, c0:c1], in_=zt[:, r, c0:c1], func=ACT.Identity, bias=negc, scale=1.0
                 )
             else:
-                nc.vector.tensor_scalar(out=zt[:, r, :], in0=zt[:, r, :], scalar1=negc, scalar2=None, op0=ALU.add)
-            nc.sync.dma_start(out=out_view[:, r, :], in_=zt[:, r, :])
+                nc.vector.tensor_scalar(
+                    out=zt[:, r, c0:c1], in0=zt[:, r, c0:c1], scalar1=negc, scalar2=None, op0=ALU.add
+                )
+
+        def store(i, c0=0, c1=N_CLS):
+            r = (i + 2) % SLOTS
+            nc.sync.dma_start(out=out_view[:, r, c0:c1], in_=zt[:, r, c0:c1])
 
         nc.scalar.dma_start(out=wsc[:], in_=W2_scale[0, :, :].rearrange("(p t) u -> p (t u)", t=4))
         load_w(0, 0, 2)
@@ -206,7 +212,7 @@ def tile_predictor_pb_kernel(tc, H, W2_bytes, W2_scale, b2, out):
         nc.vector.memset(hg[:, 0 : 2 * K_DIM], 0.0)
         nc.scalar.activation(out=warm2[:], in_=warm[:], func=ACT.Exp)
         for t in range(DEG - 1):
-            nc.gpsimd.memset(coef[:, :, t], LN_C[DEG - 2 - t])
+            nc.vector.memset(coef[:, :, t], LN_C[DEG - 2 - t])
 
         widen("s", 0, 0)
         widen("v", 0, 1)
@@ -245,25 +251,48 @@ def tile_predictor_pb_kernel(tc, H, W2_bytes, W2_scale, b2, out):
         quant_h(0, 2)
         tile_mms(3)
 
+        HALF = N_CLS // 2
+        LAST = SLOTS - 1
         add_bias(0)
+        tile_mms(4)
+        add_bias(1)
+        tile_mms(5)
         for i in range(SLOTS):
-            if i + 1 < SLOTS:
-                add_bias(i + 1)
             row_max(i)
-            if i + 4 < SLOTS:
-                tile_mms(i + 4)
-            if i >= 2:
+            if i + 2 < SLOTS:
+                add_bias(i + 2)
+            if i + 6 < SLOTS:
+                tile_mms(i + 6)
+            if 2 <= i < LAST:
                 ln_horner(i - 2)
             exp_sum(i)
-            if i >= 1:
-                ln_rest(i - 1)
-            if 0 <= i - 2 < S_FINALS:
-                final("s", i - 2)
-            ln_guess(i)
-        ln_rest(SLOTS - 1)
-        for k in range(S_FINALS, SLOTS - 2):
+            on_s = 0 <= i - 2 < S_FINALS
+            if on_s:
+                final("s", i - 2, 0, HALF)
+            if i < LAST - 2:
+                ln_guess(i, i + 1)
+            if i == LAST - 1:
+                ln_guess(LAST - 2, LAST - 1)
+            if on_s:
+                final("s", i - 2, HALF, N_CLS)
+                store(i - 2)
+            if i < LAST - 2:
+                ln_rest(i)
+            if i == LAST:
+                ln_rest(LAST - 2)
+        ln_guess(LAST - 1, LAST + 1)
+        for k in range(S_FINALS, LAST - 2):
             final("v", k)
-        ln_horner(SLOTS - 2)
-        final("v", SLOTS - 2)
-        ln_horner(SLOTS - 1)
-        final("v", SLOTS - 1)
+            store(k)
+        ln_horner(LAST - 2)
+        final("v", LAST - 2)
+        store(LAST - 2)
+        ln_rest(LAST - 1)
+        ln_rest(LAST)
+        ln_horner(LAST - 1)
+        ln_horner(LAST)
+        final("s", LAST, 0, SPLIT)
+        final("v", LAST, SPLIT, N_CLS)
+        store(LAST)
+        final("v", LAST - 1)
+        store(LAST - 1)

@@ -42,12 +42,15 @@ def tile_predictor_pb_kernel(tc, H, W2_bytes, W2_scale, b2, out):
     with ExitStack() as ctx:
         keep = ctx.enter_context(tc.tile_pool(name="keep", bufs=1))
         scrap = ctx.enter_context(tc.tile_pool(name="scrap", bufs=2))
-        ps_t = ctx.enter_context(tc.psum_pool(name="ps_t", bufs=4))
+        ps_t = ctx.enter_context(tc.psum_pool(name="ps_t", bufs=3))
+        ps_b = ctx.enter_context(tc.psum_pool(name="ps_b", bufs=1))
         ps_a = ctx.enter_context(tc.psum_pool(name="ps_a", bufs=4))
         ctx.enter_context(tc.manual_schedule())
 
         ident = keep.tile([P, P], F32, name="ident")
-        b2b = keep.tile([P, N_CLS], BF16, name="b2b")
+        ones = keep.tile([P, P], BF16, name="ones")
+        brow = keep.tile([P, N_CLS], BF16, name="brow")
+        bias3 = keep.tile([P, N_CLS], F32, name="bias3")
         wsc = keep.tile([P, 4], F32, name="wsc")
         warm = keep.tile([P, 1], F32, name="warm")
         warm2 = keep.tile([P, 1], F32, name="warm2")
@@ -146,9 +149,7 @@ def tile_predictor_pb_kernel(tc, H, W2_bytes, W2_scale, b2, out):
 
         def add_bias(i):
             r = (i + 2) % SLOTS
-            nc.vector.scalar_tensor_tensor(
-                out=zt[:, r, :], in0=b2b[:], scalar=3.0, in1=accs[i][:], op0=ALU.mult, op1=ALU.add
-            )
+            nc.vector.tensor_tensor(out=zt[:, r, :], in0=accs[i][:], in1=bias3[:], op=ALU.add)
 
         def row_max(i):
             r = (i + 2) % SLOTS
@@ -197,56 +198,59 @@ def tile_predictor_pb_kernel(tc, H, W2_bytes, W2_scale, b2, out):
             r = (i + 2) % SLOTS
             nc.sync.dma_start(out=out_view[:, r, c0:c1], in_=zt[:, r, c0:c1])
 
+        nc.vector.memset(brow[:], 0.0)
         nc.scalar.dma_start(out=wsc[:], in_=W2_scale[0, :, :].rearrange("(p t) u -> p (t u)", t=4))
         load_w(0, 0, 2)
         load_w(0, 2, 4)
+        nc.scalar.dma_start(out=brow[0:1, :], in_=b2)
         load_w(1, 0, 4)
-        load_h(0)
-        load_h(1)
         load_w(2, 0, 4)
-        load_h(2)
-        load_h(3)
-        nc.sync.dma_start(out=b2b[:], in_=b2.rearrange("o c -> (o c)").partition_broadcast(P))
+        for b in range(4):
+            load_h(b)
         nc.gpsimd.memset(warm[:], 0.0)
+        nc.gpsimd.memset(ones[:], 1.0)
         make_identity(nc, ident[:])
-        nc.vector.memset(hg[:, 0 : 2 * K_DIM], 0.0)
         nc.scalar.activation(out=warm2[:], in_=warm[:], func=ACT.Exp)
+        nc.vector.memset(hg[:, 0 : 2 * K_DIM], 0.0)
         for t in range(DEG - 1):
             nc.vector.memset(coef[:, :, t], LN_C[DEG - 2 - t])
+        bps = ps_b.tile([P, N_CLS], F32, name="bps")
+        nc.tensor.matmul(out=bps[:], lhsT=ones[:], rhs=brow[:], start=True, stop=True)
 
         widen("s", 0, 0)
         widen("v", 0, 1)
         widen("v", 0, 2)
         widen("v", 0, 3)
         widen("v", 1, 3)
-        transposes(0)
-        transposes(1)
         for t in range(3):
             widen("s", 1, t)
         interleave(0)
         widen("v", 2, 3)
-        transposes(2)
-        transposes(3)
-        evac_h(0)
-        evac_h(1)
-        interleave(1)
-        quant_w(0)
         for t in range(3):
             widen("s", 2, t)
+        transposes(0)
+        transposes(1)
+        transposes(2)
+        interleave(1)
+        quant_w(0)
+        evac_h(0)
+        transposes(3)
+        evac_h(1)
+        interleave(2)
+        nc.scalar.activation(out=bias3[:], in_=bps[:], func=ACT.Copy, scale=3.0)
         quant_h(2, 4)
         quant_w(1)
-        for i in range(3):
-            mm(i, 0, True, False)
-        for i in range(3):
-            mm(i, 1, False, False)
         evac_h(2)
+        for j in range(2):
+            for i in range(2):
+                mm(i, j, j == 0, False)
+        quant_w(2)
+        for i in range(2):
+            mm(i, 2, False, True)
         evac_h(3)
         evac_shift()
-        interleave(2)
         quant_h(6, 2)
-        quant_w(2)
-        for i in range(3):
-            mm(i, 2, False, True)
+        tile_mms(2)
         quant_h(8, 2)
         quant_h(0, 2)
         tile_mms(3)
@@ -289,8 +293,8 @@ def tile_predictor_pb_kernel(tc, H, W2_bytes, W2_scale, b2, out):
         store(LAST - 2)
         ln_rest(LAST - 1)
         ln_rest(LAST)
-        ln_horner(LAST - 1)
         ln_horner(LAST)
+        ln_horner(LAST - 1)
         final("s", LAST, 0, SPLIT)
         final("v", LAST, SPLIT, N_CLS)
         store(LAST)

@@ -30,7 +30,7 @@ LN_C = (
     0.0018373848870396614,
 )
 DEG = len(LN_C)
-S_FINALS = 3
+G_LAST = 4
 SPLIT = 192
 
 
@@ -185,7 +185,11 @@ def tile_predictor_pb_kernel(tc, H, W2_bytes, W2_scale, b2, out):
         def final(eng, i, c0=0, c1=N_CLS):
             r = (i + 2) % SLOTS
             negc = horn[:, i, DEG - 1 : DEG]
-            if eng == "s":
+            if eng == "g":
+                nc.gpsimd.tensor_scalar(
+                    out=zt[:, r, c0:c1], in0=zt[:, r, c0:c1], scalar1=1.0, scalar2=negc, op0=ALU.mult, op1=ALU.add
+                )
+            elif eng == "s":
                 nc.scalar.activation(
                     out=zt[:, r, c0:c1], in_=zt[:, r, c0:c1], func=ACT.Identity, bias=negc, scale=1.0
                 )
@@ -255,48 +259,33 @@ def tile_predictor_pb_kernel(tc, H, W2_bytes, W2_scale, b2, out):
         quant_h(0, 2)
         tile_mms(3)
 
-        HALF = N_CLS // 2
         LAST = SLOTS - 1
         add_bias(0)
         tile_mms(4)
         add_bias(1)
         tile_mms(5)
-        for i in range(SLOTS):
-            row_max(i)
+        for i in range(SLOTS + 2):
+            k = i - 2
+            if i < SLOTS:
+                row_max(i)
             if i + 2 < SLOTS:
                 add_bias(i + 2)
             if i + 6 < SLOTS:
                 tile_mms(i + 6)
-            if 2 <= i < LAST:
-                ln_horner(i - 2)
-            exp_sum(i)
-            on_s = 0 <= i - 2 < S_FINALS
-            if on_s:
-                final("s", i - 2, 0, HALF)
-            if i < LAST - 2:
+            if i < SLOTS:
+                exp_sum(i)
+            if 1 <= i <= SLOTS:
+                ln_rest(i - 1)
+            if k >= 0:
+                ln_horner(k)
+            if i < SLOTS:
                 ln_guess(i, i + 1)
-            if i == LAST - 1:
-                ln_guess(LAST - 2, LAST - 1)
-            if on_s:
-                final("s", i - 2, HALF, N_CLS)
-                store(i - 2)
-            if i < LAST - 2:
-                ln_rest(i)
-            if i == LAST:
-                ln_rest(LAST - 2)
-        ln_guess(LAST - 1, LAST + 1)
-        for k in range(S_FINALS, LAST - 2):
-            final("v", k)
-            store(k)
-        ln_horner(LAST - 2)
-        final("v", LAST - 2)
-        store(LAST - 2)
-        ln_rest(LAST - 1)
-        ln_rest(LAST)
-        ln_horner(LAST)
-        ln_horner(LAST - 1)
-        final("s", LAST, 0, SPLIT)
-        final("v", LAST, SPLIT, N_CLS)
-        store(LAST)
-        final("v", LAST - 1)
-        store(LAST - 1)
+            if 0 <= k <= G_LAST:
+                final("g", k)
+            elif G_LAST < k < LAST:
+                final("v", k)
+            elif k == LAST:
+                final("s", k, 0, SPLIT)
+                final("v", k, SPLIT, N_CLS)
+            if k >= 0:
+                store(k)

@@ -202,7 +202,7 @@ def tile_predictor_pb_kernel(tc, H, W2_bytes, W2_scale, b2, out):
             r = (i + 2) % SLOTS
             nc.sync.dma_start(out=out_view[:, r, c0:c1], in_=zt[:, r, c0:c1])
 
-        nc.vector.memset(brow[:], 0.0)
+        nc.gpsimd.memset(brow[:], 0.0)
         nc.scalar.dma_start(out=wsc[:], in_=W2_scale[0, :, :].rearrange("(p t) u -> p (t u)", t=4))
         load_w(0, 0, 2)
         load_w(0, 2, 4)
@@ -215,7 +215,7 @@ def tile_predictor_pb_kernel(tc, H, W2_bytes, W2_scale, b2, out):
         nc.gpsimd.memset(ones[:], 1.0)
         make_identity(nc, ident[:])
         nc.scalar.activation(out=warm2[:], in_=warm[:], func=ACT.Exp)
-        nc.vector.memset(hg[:, 0 : 2 * K_DIM], 0.0)
+        nc.vector.memset(hg[:, 0 : 2 * K_DIM].rearrange("p (s k) -> p s k", s=2)[:, :, 0:4], 0.0)
         for t in range(DEG - 1):
             nc.vector.memset(coef[:, :, t], LN_C[DEG - 2 - t])
         bps = ps_b.tile([P, N_CLS], F32, name="bps")

@@ -151,6 +151,14 @@ def tile_predictor_pb_kernel(tc, H, W2_bytes, W2_scale, b2, out):
             r = (i + 2) % SLOTS
             nc.vector.tensor_tensor(out=zt[:, r, :], in0=accs[i][:], in1=bias3[:], op=ALU.add)
 
+        def evac_s(i):
+            r = (i + 2) % SLOTS
+            nc.scalar.copy(out=zt[:, r, :], in_=accs[i][:])
+
+        def add_g(i):
+            r = (i + 2) % SLOTS
+            nc.gpsimd.tensor_tensor(out=zt[:, r, :], in0=zt[:, r, :], in1=bias3[:], op=ALU.add)
+
         def row_max(i):
             r = (i + 2) % SLOTS
             nc.vector.tensor_reduce(out=nmax[:, i : i + 1], in_=zt[:, r, :], axis=AX.X, op=ALU.max, negate=True)
@@ -207,8 +215,10 @@ def tile_predictor_pb_kernel(tc, H, W2_bytes, W2_scale, b2, out):
         load_w(0, 0, 2)
         load_w(0, 2, 4)
         nc.scalar.dma_start(out=brow[0:1, :], in_=b2)
-        load_w(1, 0, 4)
-        load_w(2, 0, 4)
+        load_w(1, 0, 2)
+        load_w(1, 2, 4)
+        load_w(2, 0, 2)
+        load_w(2, 2, 4)
         for b in range(4):
             load_h(b)
         nc.gpsimd.memset(warm[:], 0.0)
@@ -264,11 +274,15 @@ def tile_predictor_pb_kernel(tc, H, W2_bytes, W2_scale, b2, out):
         tile_mms(4)
         add_bias(1)
         tile_mms(5)
+        evac_s(2)
+        add_g(2)
         for i in range(SLOTS + 2):
             k = i - 2
+            if i == 2:
+                add_bias(4)
             if i < SLOTS:
                 row_max(i)
-            if i + 2 < SLOTS:
+            if i + 2 < SLOTS and i not in (0, 2):
                 add_bias(i + 2)
             if i + 6 < SLOTS:
                 tile_mms(i + 6)

@@ -245,6 +245,9 @@ def tile_predictor_pb_kernel(tc, H, W2_bytes, W2_scale, b2, out):
         transposes(0)
         transposes(1)
         transposes(2)
+        heat = ps_a.tile([P, N_CLS], F32, tag="acc", name="heat")
+        for n in range(3):
+            nc.tensor.matmul(out=heat[:], lhsT=ones[:], rhs=brow[:], start=True, stop=True)
         interleave(1)
         quant_w(0)
         evac_h(0)

@@ -210,6 +210,16 @@ def tile_predictor_pb_kernel(tc, H, W2_bytes, W2_scale, b2, out):
             r = (i + 2) % SLOTS
             nc.sync.dma_start(out=out_view[:, r, c0:c1], in_=zt[:, r, c0:c1])
 
+        heat = {}
+
+        def keep_warm(rhs):
+            if not heat:
+                heat[0] = ps_a.tile([P, N_CLS], F32, tag="acc", name="heat")
+            nc.tensor.matmul(out=heat[0][:], lhsT=ones[:], rhs=rhs, start=True, stop=True)
+
+        def plane(j, t):
+            return w_wide[j][:, t * N_CLS : (t + 1) * N_CLS]
+
         nc.gpsimd.memset(brow[:], 0.0)
         nc.scalar.dma_start(out=wsc[:], in_=W2_scale[0, :, :].rearrange("(p t) u -> p (t u)", t=4))
         load_w(0, 0, 2)
@@ -228,14 +238,16 @@ def tile_predictor_pb_kernel(tc, H, W2_bytes, W2_scale, b2, out):
         nc.vector.memset(hg[:, 0 : 2 * K_DIM].rearrange("p (s k) -> p s k", s=2)[:, :, 0:4], 0.0)
         for t in range(DEG - 1):
             nc.vector.memset(coef[:, :, t], LN_C[DEG - 2 - t])
-        bps = ps_b.tile([P, N_CLS], F32, name="bps")
-        nc.tensor.matmul(out=bps[:], lhsT=ones[:], rhs=brow[:], start=True, stop=True)
 
         widen("s", 0, 0)
         widen("v", 0, 1)
+        keep_warm(plane(0, 1))
         widen("v", 0, 2)
         widen("v", 0, 3)
         widen("v", 1, 3)
+        keep_warm(plane(1, 3))
+        bps = ps_b.tile([P, N_CLS], F32, name="bps")
+        nc.tensor.matmul(out=bps[:], lhsT=ones[:], rhs=brow[:], start=True, stop=True)
         for t in range(3):
             widen("s", 1, t)
         interleave(0)
@@ -243,17 +255,20 @@ def tile_predictor_pb_kernel(tc, H, W2_bytes, W2_scale, b2, out):
         for t in range(3):
             widen("s", 2, t)
         transposes(0)
+        keep_warm(plane(1, 1))
         transposes(1)
+        keep_warm(plane(1, 2))
         transposes(2)
-        heat = ps_a.tile([P, N_CLS], F32, tag="acc", name="heat")
-        for n in range(3):
-            nc.tensor.matmul(out=heat[:], lhsT=ones[:], rhs=brow[:], start=True, stop=True)
+        keep_warm(plane(2, 1))
+        keep_warm(plane(2, 2))
         interleave(1)
         quant_w(0)
         evac_h(0)
         transposes(3)
         evac_h(1)
+        keep_warm(hg[:, 4 * K_DIM : 5 * K_DIM])
         interleave(2)
+        keep_warm(w_grp[2][:, 0:N_CLS])
         nc.scalar.activation(out=bias3[:], in_=bps[:], func=ACT.Copy, scale=3.0)
         quant_h(2, 4)
         quant_w(1)

@@ -32,6 +32,7 @@ LN_C = (
 DEG = len(LN_C)
 G_LAST = 4
 SPLIT = 192
+CUT = 320
 
 
 def tile_predictor_pb_kernel(tc, H, W2_bytes, W2_scale, b2, out):
@@ -91,10 +92,11 @@ def tile_predictor_pb_kernel(tc, H, W2_bytes, W2_scale, b2, out):
                     out=w_wide[j][:, cols], in0=src, scalar1=wsc[:, t : t + 1], scalar2=None, op0=ALU.mult
                 )
 
-        def interleave(j):
-            nc.vector.tensor_copy(
-                out=w_grp[j][:].rearrange("p (c i t) -> p c t i", i=4, t=4),
-                in_=w_wide[j][:].rearrange("p (t c i) -> p c t i", t=4, i=4),
+        def interleave(copy, j, c0=0, c1=N_CLS):
+            blocks = slice(c0 // 4, c1 // 4)
+            copy(
+                out=w_grp[j][:].rearrange("p (c i t) -> p c t i", i=4, t=4)[:, blocks, :, :],
+                in_=w_wide[j][:].rearrange("p (t c i) -> p c t i", t=4, i=4)[:, blocks, :, :],
             )
 
         def quant_w(j):
@@ -115,10 +117,10 @@ def tile_predictor_pb_kernel(tc, H, W2_bytes, W2_scale, b2, out):
             dst = hg[:, e0 * K_DIM : (e0 + 2) * K_DIM].bitcast(F32).rearrange("p (s q u) -> p s q u", s=2, u=2)
             nc.scalar.copy(out=dst, in_=tps[b][:].rearrange("p s u q -> p s q u"))
 
-        def evac_shift():
-            dst = hg[:, 0 : 2 * K_DIM].bitcast(F32).rearrange("p (s q u) -> p s q u", s=2, u=2)
-            src = tps[3][:].rearrange("p s u q -> p s q u")
-            nc.scalar.copy(out=dst[:, :, 1:P, :], in_=src[:, :, 0 : P - 1, :])
+        def shift_slots():
+            for whole in (h_codes, h_scl):
+                slots = whole[:].rearrange("p (e q) -> p e q", q=P)
+                nc.gpsimd.tensor_copy(out=slots[:, 0:2, 1:P], in_=slots[:, SLOTS : SLOTS + 2, 0 : P - 1])
 
         def quant_h(e0, n):
             nc.vector.quantize_mx(
@@ -235,7 +237,8 @@ def tile_predictor_pb_kernel(tc, H, W2_bytes, W2_scale, b2, out):
         nc.gpsimd.memset(ones[:], 1.0)
         make_identity(nc, ident[:])
         nc.scalar.activation(out=warm2[:], in_=warm[:], func=ACT.Exp)
-        nc.vector.memset(hg[:, 0 : 2 * K_DIM].rearrange("p (s k) -> p s k", s=2)[:, :, 0:4], 0.0)
+        nc.gpsimd.memset(h_scl[:].bitcast(U32), 0)
+        nc.gpsimd.memset(h_codes[:, 0 : 2 * P : P], 0)
         for t in range(DEG - 1):
             nc.vector.memset(coef[:, :, t], LN_C[DEG - 2 - t])
 
@@ -250,7 +253,7 @@ def tile_predictor_pb_kernel(tc, H, W2_bytes, W2_scale, b2, out):
         nc.tensor.matmul(out=bps[:], lhsT=ones[:], rhs=brow[:], start=True, stop=True)
         for t in range(3):
             widen("s", 1, t)
-        interleave(0)
+        interleave(nc.vector.tensor_copy, 0)
         widen("v", 2, 3)
         for t in range(3):
             widen("s", 2, t)
@@ -261,39 +264,41 @@ def tile_predictor_pb_kernel(tc, H, W2_bytes, W2_scale, b2, out):
         transposes(2)
         keep_warm(plane(2, 1))
         keep_warm(plane(2, 2))
-        interleave(1)
+        interleave(nc.vector.tensor_copy, 1)
         quant_w(0)
         evac_h(0)
         transposes(3)
         evac_h(1)
-        keep_warm(hg[:, 4 * K_DIM : 5 * K_DIM])
-        interleave(2)
-        keep_warm(w_grp[2][:, 0:N_CLS])
-        nc.scalar.activation(out=bias3[:], in_=bps[:], func=ACT.Copy, scale=3.0)
-        quant_h(2, 4)
+        interleave(nc.vector.tensor_copy, 2, 0, CUT)
+        interleave(nc.scalar.copy, 2, CUT, N_CLS)
+        quant_h(2, 2)
+        mm(0, 0, True, False)
+        mm(1, 0, True, False)
         quant_w(1)
         evac_h(2)
-        for j in range(2):
-            for i in range(2):
-                mm(i, j, j == 0, False)
+        mm(0, 1, False, False)
+        quant_h(4, 2)
+        mm(1, 1, False, False)
+        mm(2, 0, True, False)
+        nc.scalar.activation(out=bias3[:], in_=bps[:], func=ACT.Copy, scale=3.0)
         quant_w(2)
-        for i in range(2):
-            mm(i, 2, False, True)
+        mm(0, 2, False, True)
+        mm(1, 2, False, True)
         evac_h(3)
-        evac_shift()
         quant_h(6, 2)
-        tile_mms(2)
-        quant_h(8, 2)
-        quant_h(0, 2)
-        tile_mms(3)
+        mm(2, 1, False, False)
+        mm(2, 2, False, True)
 
         LAST = SLOTS - 1
         add_bias(0)
-        tile_mms(4)
         add_bias(1)
+        quant_h(8, 2)
+        tile_mms(3)
+        tile_mms(4)
         tile_mms(5)
         evac_s(2)
         add_g(2)
+        shift_slots()
         for i in range(SLOTS + 2):
             k = i - 2
             if i == 2:

@@ -280,49 +280,81 @@ def tile_predictor_pb_kernel(tc, H, W2_bytes, W2_scale, b2, out):
         quant_h(4, 2)
         mm(1, 1, False, False)
         mm(2, 0, True, False)
-        nc.scalar.activation(out=bias3[:], in_=bps[:], func=ACT.Copy, scale=3.0)
         quant_w(2)
         mm(0, 2, False, True)
         mm(1, 2, False, True)
         evac_h(3)
+        nc.scalar.activation(out=bias3[:], in_=bps[:], func=ACT.Copy, scale=3.0)
         quant_h(6, 2)
         mm(2, 1, False, False)
         mm(2, 2, False, True)
+        quant_h(8, 2)
 
-        LAST = SLOTS - 1
         add_bias(0)
         add_bias(1)
-        quant_h(8, 2)
         tile_mms(3)
         tile_mms(4)
         tile_mms(5)
         evac_s(2)
         add_g(2)
         shift_slots()
-        for i in range(SLOTS + 2):
-            k = i - 2
-            if i == 2:
-                add_bias(4)
-            if i < SLOTS:
-                row_max(i)
-            if i + 2 < SLOTS and i not in (0, 2):
-                add_bias(i + 2)
-            if i + 6 < SLOTS:
-                tile_mms(i + 6)
-            if i < SLOTS:
-                exp_sum(i)
-            if 1 <= i <= SLOTS:
-                ln_rest(i - 1)
-            if k >= 0:
-                ln_horner(k)
-            if i < SLOTS:
-                ln_guess(i, i + 1)
-            if 0 <= k <= G_LAST:
-                final("g", k)
-            elif G_LAST < k < LAST:
-                final("v", k)
-            elif k == LAST:
-                final("s", k, 0, SPLIT)
-                final("v", k, SPLIT, N_CLS)
-            if k >= 0:
-                store(k)
+        tile_mms(6)
+        tile_mms(7)
+        row_max(0)
+        exp_sum(0)
+        row_max(1)
+        exp_sum(1)
+        add_bias(3)
+        ln_guess(0, 2)
+        add_bias(4)
+        ln_rest(0)
+        ln_rest(1)
+        row_max(2)
+        exp_sum(2)
+        row_max(3)
+        exp_sum(3)
+        ln_horner(0)
+        final("g", 0)
+        store(0)
+        ln_horner(1)
+        final("g", 1)
+        store(1)
+        row_max(4)
+        exp_sum(4)
+        add_bias(5)
+        ln_guess(2, 5)
+        add_bias(6)
+        ln_rest(2)
+        ln_rest(3)
+        ln_rest(4)
+        row_max(5)
+        exp_sum(5)
+        ln_horner(2)
+        final("g", 2)
+        store(2)
+        row_max(6)
+        exp_sum(6)
+        ln_horner(3)
+        final("g", 3)
+        store(3)
+        ln_horner(4)
+        final("g", 4)
+        store(4)
+        add_bias(7)
+        ln_guess(5, 7)
+        ln_rest(5)
+        ln_rest(6)
+        row_max(7)
+        exp_sum(7)
+        ln_horner(5)
+        final("v", 5)
+        store(5)
+        ln_horner(6)
+        final("v", 6)
+        store(6)
+        ln_guess(7, 8)
+        ln_rest(7)
+        ln_horner(7)
+        final("s", 7, 0, SPLIT)
+        final("v", 7, SPLIT, N_CLS)
+        store(7)

from contextlib import ExitStack
import math

import concourse.mybir as mybir
from concourse.masks import make_identity

N_TOK, K_DIM, N_CLS, TAPS = 1024, 512, 512, 3
FLOPS = 2 * N_TOK * K_DIM * N_CLS * TAPS

F32 = mybir.dt.float32
BF16 = mybir.dt.bfloat16
U32 = mybir.dt.uint32
U8 = mybir.dt.uint8
FP8 = mybir.dt.float8_e4m3fn
FP8X4 = mybir.dt.float8_e4m3fn_x4
ACT = mybir.ActivationFunctionType
ALU = mybir.AluOpType
AX = mybir.AxisListType

P = 128
SLOTS = 8

LN_A = math.log(2.0) / 8388608.0
LN_B = (0.043036986972427194 - 127.0) * math.log(2.0)
LN_C = (
    -1.0, 0.5, -0.3333333432674408, 0.2500000596046448, -0.19999957084655762, 0.16666363179683685,
    -0.14286194741725922, 0.12505744397640228, -0.11113137751817703, 0.09948977828025818, -0.0901292935013771,
    0.08533929288387299, -0.08288848400115967, 0.07088949531316757, -0.04805668443441391, 0.04240668565034866,
    -0.07241664826869965, 0.10330895334482193, -0.0916367769241333, 0.04873454570770264, -0.014420325867831707,
    0.0018373848870396614,
)
DEG = len(LN_C)
G_LAST = 4
SPLIT = 192
CUT = 320


def tile_predictor_pb_kernel(tc, H, W2_bytes, W2_scale, b2, out):
    nc = tc.nc
    h_view = H.rearrange("(q r) k -> q r k", r=SLOTS)
    out_view = out.rearrange("(q r) c -> q r c", r=SLOTS)

    with ExitStack() as ctx:
        keep = ctx.enter_context(tc.tile_pool(name="keep", bufs=1))
        scrap = ctx.enter_context(tc.tile_pool(name="scrap", bufs=2))
        ps_t = ctx.enter_context(tc.psum_pool(name="ps_t", bufs=3))
        ps_b = ctx.enter_context(tc.psum_pool(name="ps_b", bufs=1))
        ps_a = ctx.enter_context(tc.psum_pool(name="ps_a", bufs=4))
        ctx.enter_context(tc.manual_schedule())

        ident = keep.tile([P, P], F32, name="ident")
        ones = keep.tile([P, P], BF16, name="ones")
        brow = keep.tile([P, N_CLS], BF16, name="brow")
        bias3 = keep.tile([P, N_CLS], F32, name="bias3")
        wsc = keep.tile([P, 4], F32, name="wsc")
        warm = keep.tile([P, 1], F32, name="warm")
        warm2 = keep.tile([P, 1], F32, name="warm2")
        w_bytes = [keep.tile([P, 4 * N_CLS], U8, name="w_bytes%d" % j) for j in range(TAPS)]
        w_wide = [keep.tile([P, 4 * N_CLS], BF16, name="w_wide%d" % j) for j in range(TAPS)]
        w_grp = [keep.tile([P, 4 * N_CLS], BF16, name="w_grp%d" % j, align_bytes=64) for j in range(TAPS)]
        w_codes = [keep.tile([P, N_CLS], U32, name="w_codes%d" % j, align_bytes=64) for j in range(TAPS)]
        w_scl = [keep.tile([P, N_CLS], U8, name="w_scl%d" % j, align_bytes=64) for j in range(TAPS)]
        hs = keep.tile([P, SLOTS, K_DIM], BF16, name="hs")
        hg = keep.tile([P, (SLOTS + 2) * K_DIM], BF16, name="hg", align_bytes=64)
        h_codes = keep.tile([P, (SLOTS + 2) * P], U32, name="h_codes", align_bytes=64)
        h_scl = keep.tile([P, (SLOTS + 2) * P], U8, name="h_scl", align_bytes=64)
        zt = keep.tile([P, SLOTS, N_CLS], F32, name="zt")
        nmax = keep.tile([P, SLOTS], F32, name="nmax")
        ssum = keep.tile([P, SLOTS], F32, name="ssum")
        e_inv = keep.tile([P, SLOTS], F32, name="e_inv")
        ny0 = keep.tile([P, SLOTS], F32, name="ny0")
        u_t = keep.tile([P, SLOTS], F32, name="u_t")
        coef = keep.tile([P, SLOTS, DEG], F32, name="coef")
        horn = keep.tile([P, SLOTS, DEG], F32, name="horn")

        def load_w(j, t0, t1):
            nc.sync.dma_start(
                out=w_bytes[j][:, t0 * N_CLS : t1 * N_CLS],
                in_=W2_bytes[j, :, :].rearrange("(p t) n -> p (t n)", t=4)[:, t0 * N_CLS : t1 * N_CLS],
            )

        def load_h(b):
            nc.sync.dma_start(out=hs[:, 2 * b : 2 * b + 2, :], in_=h_view[:, 2 * b : 2 * b + 2, :])

        def widen(eng, j, t):
            cols = slice(t * N_CLS, (t + 1) * N_CLS)
            src = w_bytes[j][:, cols].bitcast(FP8)
            if eng == "s":
                nc.scalar.activation(out=w_wide[j][:, cols], in_=src, func=ACT.Copy, scale=wsc[:, t : t + 1])
            else:
                nc.vector.tensor_scalar(
                    out=w_wide[j][:, cols], in0=src, scalar1=wsc[:, t : t + 1], scalar2=None, op0=ALU.mult
                )

        def interleave(copy, j, c0=0, c1=N_CLS):
            blocks = slice(c0 // 4, c1 // 4)
            copy(
                out=w_grp[j][:].rearrange("p (c i t) -> p c t i", i=4, t=4)[:, blocks, :, :],
                in_=w_wide[j][:].rearrange("p (t c i) -> p c t i", t=4, i=4)[:, blocks, :, :],
            )

        def quant_w(j):
            nc.vector.quantize_mx(out=w_codes[j][:].bitcast(FP8X4), scales=w_scl[j][:], in_=w_grp[j][:])

        tps = {}

        def transposes(b):
            tp = ps_t.tile([P, 2, 2, P], F32, tag="tp", name="tp%d" % b)
            tps[b] = tp
            for s in range(2):
                words = hs[:, 2 * b + s, :].bitcast(F32)
                for u in range(2):
                    nc.tensor.transpose(out=tp[:, s, u, :], in_=words[:, u : K_DIM // 2 : 2], identity=ident[:])

        def evac_h(b):
            e0 = 2 + 2 * b
            dst = hg[:, e0 * K_DIM : (e0 + 2) * K_DIM].bitcast(F32).rearrange("p (s q u) -> p s q u", s=2, u=2)
            nc.scalar.copy(out=dst, in_=tps[b][:].rearrange("p s u q -> p s q u"))

        def shift_slots():
            for whole in (h_codes, h_scl):
                slots = whole[:].rearrange("p (e q) -> p e q", q=P)
                nc.gpsimd.tensor_copy(out=slots[:, 0:2, 1:P], in_=slots[:, SLOTS : SLOTS + 2, 0 : P - 1])

        def quant_h(e0, n):
            nc.vector.quantize_mx(
                out=h_codes[:, e0 * P : (e0 + n) * P].bitcast(FP8X4),
                scales=h_scl[:, e0 * P : (e0 + n) * P],
                in_=hg[:, e0 * K_DIM : (e0 + n) * K_DIM],
            )

        accs = {}

        def mm(i, j, first, last):
            if first:
                accs[i] = ps_a.tile([P, N_CLS], F32, tag="acc", name="acc%d" % i)
            e = (i + 2) % SLOTS + j
            nc.tensor.matmul_mx(
                out=accs[i][:],
                lhsT=h_codes[:, e * P : (e + 1) * P].bitcast(FP8X4),
                lhsT_scale=h_scl[:, e * P : (e + 1) * P],
                rhs=w_codes[j][:].bitcast(FP8X4),
                rhs_scale=w_scl[j][:],
                start=first,
                stop=last,
            )

        def tile_mms(i):
            for j in range(TAPS):
                mm(i, j, j == 0, j == TAPS - 1)

        def add_bias(i):
            r = (i + 2) % SLOTS
            nc.vector.tensor_tensor(out=zt[:, r, :], in0=accs[i][:], in1=bias3[:], op=ALU.add)

        def evac_s(i):
            r = (i + 2) % SLOTS
            nc.scalar.copy(out=zt[:, r, :], in_=accs[i][:])

        def add_g(i):
            r = (i + 2) % SLOTS
            nc.gpsimd.tensor_tensor(out=zt[:, r, :], in0=zt[:, r, :], in1=bias3[:], op=ALU.add)

        def row_max(i):
            r = (i + 2) % SLOTS
            nc.vector.tensor_reduce(out=nmax[:, i : i + 1], in_=zt[:, r, :], axis=AX.X, op=ALU.max, negate=True)

        def exp_sum(i):
            r = (i + 2) % SLOTS
            ex = scrap.tile([P, N_CLS], BF16, tag="ex", name="ex%d" % i)
            nc.scalar.activation(
                out=ex[:], in_=zt[:, r, :], func=ACT.Exp, bias=nmax[:, i : i + 1], scale=1.0,
                accum_out=ssum[:, i : i + 1],
            )

        def ln_guess(i0, i1):
            c = slice(i0, i1)
            bits = ssum[:, c].bitcast(U32)
            nc.scalar.activation(out=e_inv[:, c], in_=bits, func=ACT.Exp, bias=-LN_B, scale=-LN_A)
            nc.scalar.activation(out=ny0[:, c], in_=bits, func=ACT.Identity, bias=-LN_B, scale=-LN_A)

        def ln_rest(i):
            c = slice(i, i + 1)
            nc.scalar.activation(out=u_t[:, c], in_=e_inv[:, c], func=ACT.Copy, bias=-1.0, scale=ssum[:, c])
            nc.scalar.activation(
                out=coef[:, i, DEG - 1 : DEG], in_=nmax[:, c], func=ACT.Identity, bias=ny0[:, c], scale=1.0
            )

        def ln_horner(i):
            nc.vector.tensor_tensor_scan(
                out=horn[:, i, :], data0=u_t[:, i : i + 1].to_broadcast([P, DEG]), data1=coef[:, i, :],
                initial=LN_C[DEG - 1], op0=ALU.mult, op1=ALU.add,
            )

        def final(eng, i, c0=0, c1=N_CLS):
            r = (i + 2) % SLOTS
            negc = horn[:, i, DEG - 1 : DEG]
            if eng == "g":
                nc.gpsimd.tensor_scalar(
                    out=zt[:, r, c0:c1], in0=zt[:, r, c0:c1], scalar1=1.0, scalar2=negc, op0=ALU.mult, op1=ALU.add
                )
            elif eng == "s":
                nc.scalar.activation(
                    out=zt[:, r, c0:c1], in_=zt[:, r, c0:c1], func=ACT.Identity, bias=negc, scale=1.0
                )
            else:
                nc.vector.tensor_scalar(
                    out=zt[:, r, c0:c1], in0=zt[:, r, c0:c1], scalar1=negc, scalar2=None, op0=ALU.add
                )

        def store(i, c0=0, c1=N_CLS):
            r = (i + 2) % SLOTS
            nc.sync.dma_start(out=out_view[:, r, c0:c1], in_=zt[:, r, c0:c1])

        heat = {}

        def keep_warm(rhs):
            if not heat:
                heat[0] = ps_a.tile([P, N_CLS], F32, tag="acc", name="heat")
            nc.tensor.matmul(out=heat[0][:], lhsT=ones[:], rhs=rhs, start=True, stop=True)

        def plane(j, t):
            return w_wide[j][:, t * N_CLS : (t + 1) * N_CLS]

        nc.gpsimd.memset(brow[:], 0.0)
        nc.scalar.dma_start(out=wsc[:], in_=W2_scale[0, :, :].rearrange("(p t) u -> p (t u)", t=4))
        load_w(0, 0, 2)
        load_w(0, 2, 4)
        nc.scalar.dma_start(out=brow[0:1, :], in_=b2)
        load_w(1, 0, 2)
        load_w(1, 2, 4)
        load_w(2, 0, 2)
        load_w(2, 2, 4)
        for b in range(4):
            load_h(b)
        nc.gpsimd.memset(warm[:], 0.0)
        nc.gpsimd.memset(ones[:], 1.0)
        make_identity(nc, ident[:])
        nc.scalar.activation(out=warm2[:], in_=warm[:], func=ACT.Exp)
        nc.gpsimd.memset(h_scl[:].bitcast(U32), 0)
        nc.gpsimd.memset(h_codes[:, 0 : 2 * P : P], 0)
        for t in range(DEG - 1):
            nc.vector.memset(coef[:, :, t], LN_C[DEG - 2 - t])

        widen("s", 0, 0)
        widen("v", 0, 1)
        keep_warm(plane(0, 1))
        widen("v", 0, 2)
        widen("v", 0, 3)
        widen("v", 1, 3)
        keep_warm(plane(1, 3))
        bps = ps_b.tile([P, N_CLS], F32, name="bps")
        nc.tensor.matmul(out=bps[:], lhsT=ones[:], rhs=brow[:], start=True, stop=True)
        for t in range(3):
            widen("s", 1, t)
        interleave(nc.vector.tensor_copy, 0)
        widen("v", 2, 3)
        for t in range(3):
            widen("s", 2, t)
        transposes(0)
        keep_warm(plane(1, 1))
        transposes(1)
        keep_warm(plane(1, 2))
        transposes(2)
        keep_warm(plane(2, 1))
        keep_warm(plane(2, 2))
        interleave(nc.vector.tensor_copy, 1)
        quant_w(0)
        evac_h(0)
        transposes(3)
        evac_h(1)
        interleave(nc.vector.tensor_copy, 2, 0, CUT)
        interleave(nc.scalar.copy, 2, CUT, N_CLS)
        quant_h(2, 2)
        mm(0, 0, True, False)
        mm(1, 0, True, False)
        quant_w(1)
        evac_h(2)
        mm(0, 1, False, False)
        quant_h(4, 2)
        mm(1, 1, False, False)
        mm(2, 0, True, False)
        quant_w(2)
        mm(0, 2, False, True)
        mm(1, 2, False, True)
        evac_h(3)
        nc.scalar.activation(out=bias3[:], in_=bps[:], func=ACT.Copy, scale=3.0)
        quant_h(6, 2)
        mm(2, 1, False, False)
        mm(2, 2, False, True)
        quant_h(8, 2)

        add_bias(0)
        add_bias(1)
        tile_mms(3)
        tile_mms(4)
        tile_mms(5)
        evac_s(2)
        add_g(2)
        shift_slots()
        tile_mms(6)
        tile_mms(7)
        row_max(0)
        exp_sum(0)
        row_max(1)
        exp_sum(1)
        add_bias(3)
        ln_guess(0, 2)
        add_bias(4)
        ln_rest(0)
        ln_rest(1)
        row_max(2)
        exp_sum(2)
        row_max(3)
        exp_sum(3)
        ln_horner(0)
        final("g", 0)
        store(0)
        ln_horner(1)
        final("g", 1)
        store(1)
        row_max(4)
        exp_sum(4)
        add_bias(5)
        ln_guess(2, 5)
        add_bias(6)
        ln_rest(2)
        ln_rest(3)
        ln_rest(4)
        row_max(5)
        exp_sum(5)
        ln_horner(2)
        final("g", 2)
        store(2)
        row_max(6)
        exp_sum(6)
        ln_horner(3)
        final("g", 3)
        store(3)
        ln_horner(4)
        final("g", 4)
        store(4)
        add_bias(7)
        ln_guess(5, 7)
        ln_rest(5)
        ln_rest(6)
        row_max(7)
        exp_sum(7)
        ln_horner(5)
        final("v", 5)
        store(5)
        ln_horner(6)
        final("v", 6)
        store(6)
        ln_guess(7, 8)
        ln_rest(7)
        ln_horner(7)
        final("s", 7, 0, SPLIT)
        final("v", 7, SPLIT, N_CLS)
        store(7)
